import numpy as np
import ml_dtypes


def mxq(x, axis, fmt="e4m3"):
    dtype, down = {"e4m3": (ml_dtypes.float8_e4m3fn, 7), "e5m2": (ml_dtypes.float8_e5m2, 14)}[fmt]
    v = np.moveaxis(np.asarray(x, np.float32).astype(ml_dtypes.bfloat16).astype(np.float64), axis, -1)
    blocks = v.reshape(v.shape[:-1] + (-1, 32))
    amax = np.abs(blocks).max(-1, keepdims=True)
    byte = np.maximum(np.where(amax > 0, np.frexp(amax)[1] - 1 + 127, 0) - down, 1)
    scale = np.exp2(byte - 127.0)
    codes = (blocks / scale).astype(np.float32).astype(dtype).astype(np.float64)
    return np.moveaxis((codes * scale).reshape(v.shape), -1, axis)


WIDE = False


def mx_kscale(k):
    if not WIDE:
        return np.ones(k)
    levels = np.array([10, -10, 5, -5, 0])
    a = np.random.permutation(np.resize(levels, k // 512 * 4)).reshape(k // 512, 4)
    idx = np.arange(k)
    return np.exp2(a[idx // 512, idx % 128 // 32])


BF16 = ml_dtypes.bfloat16


def bf(x):
    return np.asarray(x, np.float32).astype(BF16)


def f64(x):
    return np.asarray(x).astype(np.float64)


NM, B, IN, H1, H2, OUT = 8, 512, 512, 1024, 512, 128
LS_LO, LS_HI = -20.0, 4.0


def fnoise(ei, ej):
    return np.sign(ei) * np.sign(ej) * np.sqrt(np.abs(ei)) * np.sqrt(np.abs(ej))


def plin(xq, w, b):
    y = xq.transpose(1, 0, 2) @ mxq(f64(w), 2, 'e4m3').transpose(0, 2, 1)
    return y.transpose(1, 0, 2) + f64(b)[None]


def setup_inputs():
    k = mx_kscale(IN)
    return {'s': bf(np.random.standard_normal((B, NM, IN)) * k),
            'ei1': bf(np.random.standard_normal((B, NM, 1))),
            'ej1': bf(np.random.standard_normal((1, NM, H1))),
            'w11': bf(np.random.standard_normal((NM, H1, IN)) / np.sqrt(IN) / k),
            'b11': bf(np.random.standard_normal((NM, H1)) * 0.3),
            'w12': bf(np.random.standard_normal((NM, H1, IN)) * 1.2 / np.sqrt(IN) / k),
            'b12': bf(np.random.standard_normal((NM, H1)) * 0.3)}


def reference(s, ei1, ej1, w11, b11, w12, b12):
    sq = mxq(f64(s), 2, 'e4m3')
    mu = plin(sq, w11, b11)
    log_sigma = np.clip(plin(sq, w12, b12), LS_LO, LS_HI)
    return np.maximum(mu + fnoise(f64(ei1), f64(ej1)) * np.exp(log_sigma), 0.0)

@@ -1,0 +1,345 @@
+import math
+from contextlib import ExitStack
+
+import concourse.mybir as mybir
+from concourse.masks import make_identity
+
+F32 = mybir.dt.float32
+BF16 = mybir.dt.bfloat16
+U32 = mybir.dt.uint32
+U8 = mybir.dt.uint8
+FP8X4 = mybir.dt.float8_e4m3fn_x4
+ACT = mybir.ActivationFunctionType
+ALU = mybir.AluOpType
+
+P = 128
+PACK = 4
+MODULES = 8
+ROWS = 512
+FEATURES = 512
+UNITS = 1024
+ROW_TILES = ROWS // P
+UNIT_TILES = UNITS // P
+WORDS = FEATURES // 2
+STEPS_PER_MODULE = UNIT_TILES // 2
+PAIRS = MODULES * STEPS_PER_MODULE
+
+SIGMA_MAX = math.exp(4.0)
+SIGMA_MIN = math.exp(-20.0)
+SQRT_MIN = 2.0**-116
+
+UNIT_COLUMNS = MODULES * UNIT_TILES
+ROW_COLUMNS = ROW_TILES * MODULES
+
+TRANSPOSE_AHEAD = 4
+COPY_AHEAD = 3
+QUANTISE_AHEAD = 2
+BACK_BEHIND = 1
+RELU_BEHIND = 2
+LOAD_AHEAD = 6
+
+FLOPS = 2 * 2 * MODULES * ROWS * UNITS * FEATURES
+
+
+def tile_skill_net_pa_t_kernel(tc, s, ei1, ej1, w11, b11, w12, b12, out):
+    nc = tc.nc
+
+    s_view = s.rearrange("(n a) j k -> n a j k", a=ROW_TILES)
+    w_views = [w.rearrange("j (g m) k -> j m g k", m=P) for w in (w12, w11)]
+    out_view = out.rearrange("(n a) j l -> n a j l", a=ROW_TILES)
+
+    with ExitStack() as stack:
+        const = stack.enter_context(tc.tile_pool(name="const", bufs=1))
+        raw_weights = stack.enter_context(tc.tile_pool(name="raw_weights", bufs=LOAD_AHEAD + 2))
+        raw_rows = stack.enter_context(tc.tile_pool(name="raw_rows", bufs=3))
+        grouped = stack.enter_context(tc.tile_pool(name="grouped", bufs=3))
+        packed = stack.enter_context(tc.tile_pool(name="packed", bufs=4))
+        work = stack.enter_context(tc.tile_pool(name="work", bufs=3))
+        result = stack.enter_context(tc.tile_pool(name="result", bufs=4))
+        psum = stack.enter_context(tc.psum_pool(name="psum", bufs=2))
+        stack.enter_context(tc.manual_schedule())
+
+        weight_words = {}
+        row_words = {}
+        forward_bank = {}
+        weight_grouped = {}
+        row_grouped = {}
+        weight_codes = {}
+        weight_scales = {}
+        row_codes = {}
+        row_scales = {}
+        row_factor = {}
+        log_sigma_bank = {}
+        mu_bank = {}
+        sigma = {}
+        summed = {}
+        backward_bank = {}
+        out_pair = {}
+
+        def load_rows(j):
+            s_raw = raw_rows.tile([P, ROW_TILES * FEATURES], BF16, name="s_raw")
+            nc.sync.dma_start(
+                out=s_raw[:].rearrange("p (a k) -> p a k", a=ROW_TILES), in_=s_view[:, :, j, :]
+            )
+            row_words[j] = s_raw[:].bitcast(F32)
+
+        def load_weights(q):
+            j, first_tile = q // STEPS_PER_MODULE, 2 * (q % STEPS_PER_MODULE)
+            w_raw = raw_weights.tile([P, 2 * 2 * FEATURES], BF16, name="w_raw")
+            for x in range(2):
+                nc.sync.dma_start(
+                    out=w_raw[:, x * 2 * FEATURES : (x + 1) * 2 * FEATURES].rearrange(
+                        "p (t k) -> p t k", t=2
+                    ),
+                    in_=w_views[x][j, :, first_tile : first_tile + 2, :],
+                )
+            weight_words[q] = w_raw[:].bitcast(F32)
+
+        def load_for_pair(q):
+            if q % STEPS_PER_MODULE == 0:
+                load_rows(q // STEPS_PER_MODULE)
+            load_weights(q)
+
+        def transpose_two_tiles(words, first_word, key):
+            bank = psum.tile([P, 2, 2, P], F32, name="forward", tag="forward")
+            for t in range(2):
+                for u in range(2):
+                    start = first_word + t * WORDS + u * P
+                    nc.tensor.transpose(bank[:, t, u, :], words[:, start : start + P], ident[:])
+            forward_bank[key] = bank
+
+        def side_by_side(copy, key, grouped_words):
+            copy(out=grouped_words, in_=forward_bank[key][:].rearrange("p t u r -> p t r u"))
+
+        def transpose_weights(q, x):
+            transpose_two_tiles(weight_words[q], x * 2 * WORDS, ("w", q, x))
+
+        def copy_weights(q, x):
+            if x == 0:
+                weight_grouped[q] = grouped.tile(
+                    [P, 2 * 2 * P * PACK], BF16, name="w_grouped", align_bytes=64
+                )
+            view = weight_grouped[q][:].bitcast(F32).rearrange(
+                "p (x t m u) -> p x t m u", x=2, t=2, u=2
+            )
+            side_by_side(nc.scalar.copy, ("w", q, x), view[:, x])
+
+        def quantise_weights(q):
+            weight_codes[q] = packed.tile([P, 2 * 2 * P], U32, name="w_codes", align_bytes=64)
+            weight_scales[q] = packed.tile([P, 2 * 2 * P], U8, name="w_scales", align_bytes=64)
+            nc.vector.quantize_mx(
+                out=weight_codes[q][:].bitcast(FP8X4),
+                scales=weight_scales[q][:],
+                in_=weight_grouped[q][:],
+            )
+
+        def transpose_rows(j, half):
+            transpose_two_tiles(row_words[j], half * 2 * WORDS, ("s", j, half))
+
+        def copy_rows(j, half):
+            if half == 0:
+                row_grouped[j] = grouped.tile([P, ROWS * PACK], BF16, name="s_grouped", align_bytes=64)
+            view = row_grouped[j][:].bitcast(F32).rearrange("p (a n u) -> p a n u", a=ROW_TILES, u=2)
+            side_by_side(nc.vector.tensor_copy, ("s", j, half), view[:, 2 * half : 2 * half + 2])
+
+        def quantise_rows(j):
+            row_codes[j] = packed.tile([P, ROWS], U32, name="s_codes", align_bytes=64)
+            row_scales[j] = packed.tile([P, ROWS], U8, name="s_scales", align_bytes=64)
+            nc.vector.quantize_mx(
+                out=row_codes[j][:].bitcast(FP8X4),
+                scales=row_scales[j][:],
+                in_=row_grouped[j][:],
+            )
+
+        def spread_row_factor(j):
+            bank = psum.tile([P, ROW_TILES, P], F32, name="forward", tag="forward")
+            for a in range(ROW_TILES):
+                column = UNIT_COLUMNS + a * MODULES + j
+                nc.tensor.transpose(
+                    bank[:, a, :], factor[:, column : column + 1].to_broadcast([P, P]), ident[:]
+                )
+            forward_bank[("f", j)] = bank
+
+        def copy_row_factor(j):
+            row_factor[j] = work.tile([P, ROWS], F32, name="row_factor")
+            nc.vector.tensor_copy(
+                out=row_factor[j][:], in_=forward_bank[("f", j)][:].rearrange("p a n -> p (a n)")
+            )
+
+        def multiply(q, x, banks, tag):
+            j = q // STEPS_PER_MODULE
+            for t in range(2):
+                bank = psum.tile([P, ROWS], F32, name=tag, tag=tag)
+                tile_columns = slice((2 * x + t) * P, (2 * x + t + 1) * P)
+                nc.tensor.matmul_mx(
+                    out=bank[:],
+                    lhsT=weight_codes[q][:, tile_columns].bitcast(FP8X4),
+                    lhsT_scale=weight_scales[q][:, tile_columns],
+                    rhs=row_codes[j][:].bitcast(FP8X4),
+                    rhs_scale=row_scales[j][:],
+                    start=True,
+                    stop=True,
+                )
+                banks[(q, t)] = bank
+
+        def exponentials(q):
+            sigma[q] = work.tile([P, 2, ROWS], F32, name="sigma")
+            for t in range(2):
+                nc.scalar.activation(
+                    out=sigma[q][:, t, :],
+                    in_=log_sigma_bank[(q, t)][:],
+                    func=ACT.Exp,
+                    bias=b12_columns[:, 2 * q + t : 2 * q + t + 1],
+                    scale=1.0,
+                )
+
+        def clip_sigma(q):
+            for t in range(2):
+                nc.gpsimd.tensor_scalar(
+                    out=sigma[q][:, t, :],
+                    in0=sigma[q][:, t, :],
+                    scalar1=SIGMA_MAX,
+                    scalar2=SIGMA_MIN,
+                    op0=ALU.min,
+                    op1=ALU.max,
+                )
+
+        def scale_noise(q):
+            for t in range(2):
+                nc.vector.scalar_tensor_tensor(
+                    out=sigma[q][:, t, :],
+                    in0=sigma[q][:, t, :],
+                    scalar=factor[:, 2 * q + t : 2 * q + t + 1],
+                    in1=row_factor[q // STEPS_PER_MODULE][:],
+                    op0=ALU.mult,
+                    op1=ALU.mult,
+                )
+
+        def add_mu(q):
+            summed[q] = work.tile([P, 2, ROWS], F32, name="summed")
+            for t in range(2):
+                nc.vector.scalar_tensor_tensor(
+                    out=summed[q][:, t, :],
+                    in0=mu_bank[(q, t)][:],
+                    scalar=b11_columns[:, 2 * q + t : 2 * q + t + 1],
+                    in1=sigma[q][:, t, :],
+                    op0=ALU.add,
+                    op1=ALU.add,
+                )
+
+        def transpose_back(q, t):
+            bank = psum.tile([P, ROW_TILES, P], F32, name="backward", tag="backward")
+            for a in range(ROW_TILES):
+                nc.tensor.transpose(bank[:, a, :], summed[q][:, t, a * P : (a + 1) * P], ident[:])
+            backward_bank[(q, t)] = bank
+
+        def relu_out(q, t, on_vector):
+            if t == 0:
+                out_pair[q] = result.tile([P, ROW_TILES, 2 * P], F32, name="out_pair")
+            out_tile = out_pair[q][:, :, t * P : (t + 1) * P]
+            if on_vector:
+                nc.vector.tensor_scalar_max(out=out_tile, in0=backward_bank[(q, t)][:], scalar1=0.0)
+            else:
+                nc.scalar.activation(out=out_tile, in_=backward_bank[(q, t)][:], func=ACT.Relu)
+
+        def store(q):
+            j, first_unit = q // STEPS_PER_MODULE, 2 * P * (q % STEPS_PER_MODULE)
+            nc.sync.dma_start(
+                out=out_view[:, :, j, first_unit : first_unit + 2 * P], in_=out_pair[q][:]
+            )
+
+        ident = const.tile([P, P], F32, name="ident")
+        make_identity(nc, ident[:])
+
+        lines_bf16 = const.tile([P, 2, P], BF16, name="lines_bf16")
+        nc.vector.memset(lines_bf16[:], 0.0)
+        ei_bf16 = const.tile([P, ROW_COLUMNS], BF16, name="ei_bf16")
+        nc.sync.dma_start(out=ei_bf16[:], in_=ei1.rearrange("(n a) j o -> n (a j o)", a=ROW_TILES))
+        nc.sync.dma_start(
+            out=lines_bf16[0:UNIT_COLUMNS, 1, :], in_=ej1.rearrange("o j (g m) -> (o j g) m", m=P)
+        )
+        nc.sync.dma_start(out=lines_bf16[0:UNIT_COLUMNS, 0, :], in_=b11.rearrange("j (g m) -> (j g) m", m=P))
+        nc.sync.dma_start(out=lines_bf16[UNIT_COLUMNS:P, 0, :], in_=b12.rearrange("j (g m) -> (j g) m", m=P))
+        for q in range(LOAD_AHEAD):
+            load_for_pair(q)
+
+        lines_f32 = const.tile([P, 2, P], F32, name="lines_f32")
+        nc.vector.tensor_copy(out=lines_f32[:], in_=lines_bf16[:])
+        column_bank = psum.tile([P, 2, P], F32, name="forward", tag="forward")
+        for sheet in range(2):
+            nc.tensor.transpose(column_bank[:, sheet, :], lines_f32[:, sheet, :], ident[:])
+        b11_columns = const.tile([P, UNIT_COLUMNS], F32, name="b11_columns")
+        nc.vector.tensor_copy(out=b11_columns[:], in_=column_bank[:, 0, 0:UNIT_COLUMNS])
+        b12_columns = const.tile([P, UNIT_COLUMNS], F32, name="b12_columns")
+        nc.vector.tensor_copy(out=b12_columns[:], in_=column_bank[:, 0, UNIT_COLUMNS:P])
+
+        draws = const.tile([P, UNIT_COLUMNS + ROW_COLUMNS], F32, name="draws")
+        nc.vector.tensor_copy(out=draws[:, 0:UNIT_COLUMNS], in_=column_bank[:, 1, 0:UNIT_COLUMNS])
+        nc.vector.tensor_copy(out=draws[:, UNIT_COLUMNS:], in_=ei_bf16[:])
+        magnitude = const.tile([P, UNIT_COLUMNS + ROW_COLUMNS], F32, name="magnitude")
+        nc.vector.scalar_tensor_tensor(
+            out=magnitude[:], in0=draws[:], scalar=-1.0, in1=draws[:], op0=ALU.mult, op1=ALU.max
+        )
+        lifted = const.tile([P, UNIT_COLUMNS + ROW_COLUMNS], F32, name="lifted")
+        nc.vector.tensor_scalar_max(out=lifted[:], in0=magnitude[:], scalar1=SQRT_MIN)
+        root = const.tile([P, UNIT_COLUMNS + ROW_COLUMNS], F32, name="root")
+        nc.scalar.activation(out=root[:], in_=lifted[:], func=ACT.Sqrt)
+        signs = const.tile([P, UNIT_COLUMNS + ROW_COLUMNS], F32, name="signs")
+        nc.scalar.activation(out=signs[:], in_=draws[:], func=ACT.Sign)
+        factor = const.tile([P, UNIT_COLUMNS + ROW_COLUMNS], F32, name="factor")
+        nc.vector.tensor_mul(out=factor[:], in0=signs[:], in1=root[:])
+
+        for q in range(-TRANSPOSE_AHEAD, PAIRS + RELU_BEHIND):
+            step_in_module = q % STEPS_PER_MODULE
+            coming = q // STEPS_PER_MODULE + 1
+            extra_rows = coming < MODULES and step_in_module < 2
+            extra_factor = coming < MODULES and step_in_module == 3
+            vector_is_done = q >= PAIRS
+
+            if q + TRANSPOSE_AHEAD + LOAD_AHEAD < PAIRS:
+                load_for_pair(q + TRANSPOSE_AHEAD + LOAD_AHEAD)
+
+            if 0 <= q < PAIRS:
+                exponentials(q)
+                clip_sigma(q)
+            if 0 <= q + 1 < PAIRS:
+                multiply(q + 1, 0, log_sigma_bank, "log_sigma")
+
+            if 0 <= q + COPY_AHEAD < PAIRS:
+                copy_weights(q + COPY_AHEAD, 0)
+            if extra_rows:
+                transpose_rows(coming, step_in_module)
+            if extra_factor:
+                spread_row_factor(coming)
+            if 0 <= q - RELU_BEHIND < PAIRS:
+                relu_out(q - RELU_BEHIND, 0, False)
+            if 0 <= q - BACK_BEHIND < PAIRS:
+                transpose_back(q - BACK_BEHIND, 0)
+            if 0 <= q + COPY_AHEAD < PAIRS:
+                copy_weights(q + COPY_AHEAD, 1)
+            if q + TRANSPOSE_AHEAD < PAIRS:
+                transpose_weights(q + TRANSPOSE_AHEAD, 0)
+
+            if 0 <= q < PAIRS:
+                multiply(q, 1, mu_bank, "mu")
+
+            if 0 <= q - RELU_BEHIND < PAIRS:
+                relu_out(q - RELU_BEHIND, 1, vector_is_done)
+                store(q - RELU_BEHIND)
+            if 0 <= q - BACK_BEHIND < PAIRS:
+                transpose_back(q - BACK_BEHIND, 1)
+
+            if 0 <= q + QUANTISE_AHEAD < PAIRS:
+                quantise_weights(q + QUANTISE_AHEAD)
+            if coming < MODULES and step_in_module == 2:
+                quantise_rows(coming)
+            if 0 <= q < PAIRS:
+                scale_noise(q)
+            if extra_rows:
+                copy_rows(coming, step_in_module)
+            if extra_factor:
+                copy_row_factor(coming)
+            if q + TRANSPOSE_AHEAD < PAIRS:
+                transpose_weights(q + TRANSPOSE_AHEAD, 1)
+            if 0 <= q < PAIRS:
+                add_mu(q)

@@ -45,7 +45,7 @@ def tile_skill_net_pa_t_kernel(tc, s, ei1, ej1, w11, b11, w12, b12, out):
     nc = tc.nc
 
     s_view = s.rearrange("(n a) j k -> n a j k", a=ROW_TILES)
-    w_views = [w.rearrange("j (g m) k -> j m g k", m=P) for w in (w12, w11)]
+    w_views = [w.rearrange("j (r m t) k -> j r m t k", m=P, t=2) for w in (w12, w11)]
     out_view = out.rearrange("(n a) j l -> n a j l", a=ROW_TILES)
 
     with ExitStack() as stack:
@@ -76,43 +76,47 @@ def tile_skill_net_pa_t_kernel(tc, s, ei1, ej1, w11, b11, w12, b12, out):
         backward_bank = {}
         out_pair = {}
 
-        def load_rows(j):
-            s_raw = raw_rows.tile([P, ROW_TILES * FEATURES], BF16, name="s_raw")
+        def load_rows(first, count):
+            s_raw = raw_rows.tile([P, ROW_TILES, 2 * FEATURES], BF16, name="s_raw")
             nc.sync.dma_start(
-                out=s_raw[:].rearrange("p (a k) -> p a k", a=ROW_TILES), in_=s_view[:, :, j, :]
+                out=s_raw[:, :, 0 : count * FEATURES],
+                in_=s_view[:, :, first : first + count, :].rearrange("n a j k -> n a (j k)"),
             )
-            row_words[j] = s_raw[:].bitcast(F32)
+            for j in range(count):
+                row_words[first + j] = s_raw[:].bitcast(F32)[:, :, j * WORDS : (j + 1) * WORDS]
 
         def load_weights(q):
-            j, first_tile = q // STEPS_PER_MODULE, 2 * (q % STEPS_PER_MODULE)
+            j, r = q // STEPS_PER_MODULE, q % STEPS_PER_MODULE
             w_raw = raw_weights.tile([P, 2 * 2 * FEATURES], BF16, name="w_raw")
             for x in range(2):
                 nc.sync.dma_start(
                     out=w_raw[:, x * 2 * FEATURES : (x + 1) * 2 * FEATURES].rearrange(
                         "p (t k) -> p t k", t=2
                     ),
-                    in_=w_views[x][j, :, first_tile : first_tile + 2, :],
+                    in_=w_views[x][j, r],
                 )
             weight_words[q] = w_raw[:].bitcast(F32)
 
         def load_for_pair(q):
-            if q % STEPS_PER_MODULE == 0:
-                load_rows(q // STEPS_PER_MODULE)
+            if q == 0:
+                load_rows(0, 1)
+            elif q == 2:
+                load_rows(1, 1)
+            elif q % (2 * STEPS_PER_MODULE) == STEPS_PER_MODULE and q < PAIRS - STEPS_PER_MODULE:
+                load_rows(q // STEPS_PER_MODULE + 1, 2)
             load_weights(q)
 
-        def transpose_two_tiles(words, first_word, key):
+        def transpose_two_tiles(tiles, key):
             bank = psum.tile([P, 2, 2, P], F32, name="forward", tag="forward")
             for t in range(2):
                 for u in range(2):
-                    start = first_word + t * WORDS + u * P
-                    nc.tensor.transpose(bank[:, t, u, :], words[:, start : start + P], ident[:])
+                    nc.tensor.transpose(bank[:, t, u, :], tiles[t][:, u * P : (u + 1) * P], ident[:])
             forward_bank[key] = bank
 
-        def side_by_side(copy, key, grouped_words):
-            copy(out=grouped_words, in_=forward_bank[key][:].rearrange("p t u r -> p t r u"))
-
         def transpose_weights(q, x):
-            transpose_two_tiles(weight_words[q], x * 2 * WORDS, ("w", q, x))
+            first = 2 * x * WORDS
+            tiles = [weight_words[q][:, first + t * WORDS : first + (t + 1) * WORDS] for t in range(2)]
+            transpose_two_tiles(tiles, ("w", q, x))
 
         def copy_weights(q, x):
             if x == 0:
@@ -120,9 +124,11 @@ def tile_skill_net_pa_t_kernel(tc, s, ei1, ej1, w11, b11, w12, b12, out):
                     [P, 2 * 2 * P * PACK], BF16, name="w_grouped", align_bytes=64
                 )
             view = weight_grouped[q][:].bitcast(F32).rearrange(
-                "p (x t m u) -> p x t m u", x=2, t=2, u=2
+                "p (x m t u) -> p x m t u", x=2, t=2, u=2
             )
-            side_by_side(nc.scalar.copy, ("w", q, x), view[:, x])
+            nc.scalar.copy(
+                out=view[:, x], in_=forward_bank[("w", q, x)][:].rearrange("p t u m -> p m t u")
+            )
 
         def quantise_weights(q):
             weight_codes[q] = packed.tile([P, 2 * 2 * P], U32, name="w_codes", align_bytes=64)
@@ -134,13 +140,17 @@ def tile_skill_net_pa_t_kernel(tc, s, ei1, ej1, w11, b11, w12, b12, out):
             )
 
         def transpose_rows(j, half):
-            transpose_two_tiles(row_words[j], half * 2 * WORDS, ("s", j, half))
+            tiles = [row_words[j][:, 2 * half + t, :] for t in range(2)]
+            transpose_two_tiles(tiles, ("s", j, half))
 
         def copy_rows(j, half):
             if half == 0:
                 row_grouped[j] = grouped.tile([P, ROWS * PACK], BF16, name="s_grouped", align_bytes=64)
             view = row_grouped[j][:].bitcast(F32).rearrange("p (a n u) -> p a n u", a=ROW_TILES, u=2)
-            side_by_side(nc.vector.tensor_copy, ("s", j, half), view[:, 2 * half : 2 * half + 2])
+            nc.vector.tensor_copy(
+                out=view[:, 2 * half : 2 * half + 2],
+                in_=forward_bank[("s", j, half)][:].rearrange("p t u r -> p t r u"),
+            )
 
         def quantise_rows(j):
             row_codes[j] = packed.tile([P, ROWS], U32, name="s_codes", align_bytes=64)
@@ -234,18 +244,25 @@ def tile_skill_net_pa_t_kernel(tc, s, ei1, ej1, w11, b11, w12, b12, out):
             backward_bank[(q, t)] = bank
 
         def relu_out(q, t, on_vector):
-            if t == 0:
-                out_pair[q] = result.tile([P, ROW_TILES, 2 * P], F32, name="out_pair")
-            out_tile = out_pair[q][:, :, t * P : (t + 1) * P]
+            if t == 0 and q % 2 == 0:
+                out_pair[q // 2] = result.tile([P, ROW_TILES, 4 * P], F32, name="out_pair")
+            first = (2 * (q % 2) + t) * P
+            out_tile = out_pair[q // 2][:, :, first : first + P]
             if on_vector:
                 nc.vector.tensor_scalar_max(out=out_tile, in0=backward_bank[(q, t)][:], scalar1=0.0)
             else:
                 nc.scalar.activation(out=out_tile, in_=backward_bank[(q, t)][:], func=ACT.Relu)
 
         def store(q):
-            j, first_unit = q // STEPS_PER_MODULE, 2 * P * (q % STEPS_PER_MODULE)
+            one_by_one = q >= PAIRS - 2
+            if q % 2 == 0 and not one_by_one:
+                return
+            width = 2 * P if one_by_one else 4 * P
+            last = 2 * P * (q % 2) + 2 * P
+            j, last_unit = q // STEPS_PER_MODULE, 2 * P * (q % STEPS_PER_MODULE) + 2 * P
             nc.sync.dma_start(
-                out=out_view[:, :, j, first_unit : first_unit + 2 * P], in_=out_pair[q][:]
+                out=out_view[:, :, j, last_unit - width : last_unit],
+                in_=out_pair[q // 2][:, :, last - width : last],
             )
 
         ident = const.tile([P, P], F32, name="ident")

@@ -68,7 +68,6 @@ def tile_skill_net_pa_t_kernel(tc, s, ei1, ej1, w11, b11, w12, b12, out):
         weight_scales = {}
         row_codes = {}
         row_scales = {}
-        row_factor = {}
         log_sigma_bank = {}
         mu_bank = {}
         sigma = {}
@@ -85,6 +84,13 @@ def tile_skill_net_pa_t_kernel(tc, s, ei1, ej1, w11, b11, w12, b12, out):
             for j in range(count):
                 row_words[first + j] = s_raw[:].bitcast(F32)[:, :, j * WORDS : (j + 1) * WORDS]
 
+        def load_first_rows():
+            s_raw = raw_rows.tile([P, ROW_TILES, 2 * FEATURES], BF16, name="s_raw")
+            for half in range(2):
+                tiles = slice(2 * half, 2 * half + 2)
+                nc.sync.dma_start(out=s_raw[:, tiles, 0:FEATURES], in_=s_view[:, tiles, 0, :])
+            row_words[0] = s_raw[:].bitcast(F32)[:, :, 0:WORDS]
+
         def load_weights(q):
             j, r = q // STEPS_PER_MODULE, q % STEPS_PER_MODULE
             w_raw = raw_weights.tile([P, 2 * 2 * FEATURES], BF16, name="w_raw")
@@ -98,16 +104,14 @@ def tile_skill_net_pa_t_kernel(tc, s, ei1, ej1, w11, b11, w12, b12, out):
             weight_words[q] = w_raw[:].bitcast(F32)
 
         def load_for_pair(q):
-            if q == 0:
-                load_rows(0, 1)
-            elif q == 2:
+            if q == 2:
                 load_rows(1, 1)
             elif q % (2 * STEPS_PER_MODULE) == STEPS_PER_MODULE and q < PAIRS - STEPS_PER_MODULE:
                 load_rows(q // STEPS_PER_MODULE + 1, 2)
             load_weights(q)
 
-        def transpose_two_tiles(tiles, key):
-            bank = psum.tile([P, 2, 2, P], F32, name="forward", tag="forward")
+        def transpose_two_tiles(tiles, key, tag="forward"):
+            bank = psum.tile([P, 2, 2, P], F32, name=tag, tag=tag)
             for t in range(2):
                 for u in range(2):
                     nc.tensor.transpose(bank[:, t, u, :], tiles[t][:, u * P : (u + 1) * P], ident[:])
@@ -139,9 +143,9 @@ def tile_skill_net_pa_t_kernel(tc, s, ei1, ej1, w11, b11, w12, b12, out):
                 in_=weight_grouped[q][:],
             )
 
-        def transpose_rows(j, half):
+        def transpose_rows(j, half, tag="forward"):
             tiles = [row_words[j][:, 2 * half + t, :] for t in range(2)]
-            transpose_two_tiles(tiles, ("s", j, half))
+            transpose_two_tiles(tiles, ("s", j, half), tag)
 
         def copy_rows(j, half):
             if half == 0:
@@ -161,20 +165,28 @@ def tile_skill_net_pa_t_kernel(tc, s, ei1, ej1, w11, b11, w12, b12, out):
                 in_=row_grouped[j][:],
             )
 
-        def spread_row_factor(j):
+        def spread_first_row_factor():
             bank = psum.tile([P, ROW_TILES, P], F32, name="forward", tag="forward")
             for a in range(ROW_TILES):
-                column = UNIT_COLUMNS + a * MODULES + j
+                column = UNIT_COLUMNS + a
                 nc.tensor.transpose(
                     bank[:, a, :], factor[:, column : column + 1].to_broadcast([P, P]), ident[:]
                 )
-            forward_bank[("f", j)] = bank
+            forward_bank["f"] = bank
 
-        def copy_row_factor(j):
-            row_factor[j] = work.tile([P, ROWS], F32, name="row_factor")
+        def copy_first_row_factor():
             nc.vector.tensor_copy(
-                out=row_factor[j][:], in_=forward_bank[("f", j)][:].rearrange("p a n -> p (a n)")
+                out=row_factor[:, 0:ROWS], in_=forward_bank["f"][:].rearrange("p a n -> p (a n)")
             )
+
+        def spread_other_row_factors():
+            bank = psum.tile([P, P], F32, name="backward", tag="backward")
+            nc.tensor.transpose(bank[:], factor[:], ident[:])
+            line_pieces = const.tile([P, P], F32, name="line_pieces")
+            pieces = slice(UNIT_COLUMNS, UNIT_COLUMNS + ROW_COLUMNS)
+            nc.vector.tensor_copy(out=line_pieces[pieces, :], in_=bank[pieces, :])
+            nc.sync.dma_start(out=parked.rearrange("(c n) -> c n", n=P), in_=line_pieces[pieces, :])
+            nc.sync.dma_start(out=row_factor[:, ROWS:], in_=parked[ROWS:].partition_broadcast(P))
 
         def multiply(q, x, banks, tag):
             j = q // STEPS_PER_MODULE
@@ -215,12 +227,13 @@ def tile_skill_net_pa_t_kernel(tc, s, ei1, ej1, w11, b11, w12, b12, out):
                 )
 
         def scale_noise(q):
+            j = q // STEPS_PER_MODULE
             for t in range(2):
                 nc.vector.scalar_tensor_tensor(
                     out=sigma[q][:, t, :],
                     in0=sigma[q][:, t, :],
                     scalar=factor[:, 2 * q + t : 2 * q + t + 1],
-                    in1=row_factor[q // STEPS_PER_MODULE][:],
+                    in1=row_factor[:, j * ROWS : (j + 1) * ROWS],
                     op0=ALU.mult,
                     op1=ALU.mult,
                 )
@@ -268,53 +281,67 @@ def tile_skill_net_pa_t_kernel(tc, s, ei1, ej1, w11, b11, w12, b12, out):
         ident = const.tile([P, P], F32, name="ident")
         make_identity(nc, ident[:])
 
-        lines_bf16 = const.tile([P, 2, P], BF16, name="lines_bf16")
-        nc.vector.memset(lines_bf16[:], 0.0)
-        ei_bf16 = const.tile([P, ROW_COLUMNS], BF16, name="ei_bf16")
-        nc.sync.dma_start(out=ei_bf16[:], in_=ei1.rearrange("(n a) j o -> n (a j o)", a=ROW_TILES))
-        nc.sync.dma_start(
-            out=lines_bf16[0:UNIT_COLUMNS, 1, :], in_=ej1.rearrange("o j (g m) -> (o j g) m", m=P)
-        )
-        nc.sync.dma_start(out=lines_bf16[0:UNIT_COLUMNS, 0, :], in_=b11.rearrange("j (g m) -> (j g) m", m=P))
-        nc.sync.dma_start(out=lines_bf16[UNIT_COLUMNS:P, 0, :], in_=b12.rearrange("j (g m) -> (j g) m", m=P))
+        draws = const.tile([P, P + ROW_COLUMNS], BF16, name="draws")
+        nc.vector.memset(draws[:], 0.0)
+        lines_bf16 = const.tile([P, P], BF16, name="lines_bf16")
+        nc.sync.dma_start(out=draws[0:UNIT_COLUMNS, 0:P], in_=ej1.rearrange("o j (g m) -> (o j g) m", m=P))
+        nc.sync.dma_start(out=draws[:, P:], in_=ei1.rearrange("(n a) j o -> n (a j o)", a=ROW_TILES))
+        load_first_rows()
+        nc.sync.dma_start(out=lines_bf16[0:UNIT_COLUMNS, :], in_=b11.rearrange("j (g m) -> (j g) m", m=P))
+        nc.sync.dma_start(out=lines_bf16[UNIT_COLUMNS:P, :], in_=b12.rearrange("j (g m) -> (j g) m", m=P))
         for q in range(LOAD_AHEAD):
             load_for_pair(q)
 
-        lines_f32 = const.tile([P, 2, P], F32, name="lines_f32")
-        nc.vector.tensor_copy(out=lines_f32[:], in_=lines_bf16[:])
-        column_bank = psum.tile([P, 2, P], F32, name="forward", tag="forward")
-        for sheet in range(2):
-            nc.tensor.transpose(column_bank[:, sheet, :], lines_f32[:, sheet, :], ident[:])
-        b11_columns = const.tile([P, UNIT_COLUMNS], F32, name="b11_columns")
-        nc.vector.tensor_copy(out=b11_columns[:], in_=column_bank[:, 0, 0:UNIT_COLUMNS])
-        b12_columns = const.tile([P, UNIT_COLUMNS], F32, name="b12_columns")
-        nc.vector.tensor_copy(out=b12_columns[:], in_=column_bank[:, 0, UNIT_COLUMNS:P])
-
-        draws = const.tile([P, UNIT_COLUMNS + ROW_COLUMNS], F32, name="draws")
-        nc.vector.tensor_copy(out=draws[:, 0:UNIT_COLUMNS], in_=column_bank[:, 1, 0:UNIT_COLUMNS])
-        nc.vector.tensor_copy(out=draws[:, UNIT_COLUMNS:], in_=ei_bf16[:])
-        magnitude = const.tile([P, UNIT_COLUMNS + ROW_COLUMNS], F32, name="magnitude")
+        magnitude = const.tile([P, P + ROW_COLUMNS], F32, name="magnitude")
         nc.vector.scalar_tensor_tensor(
             out=magnitude[:], in0=draws[:], scalar=-1.0, in1=draws[:], op0=ALU.mult, op1=ALU.max
         )
-        lifted = const.tile([P, UNIT_COLUMNS + ROW_COLUMNS], F32, name="lifted")
+        lifted = const.tile([P, P + ROW_COLUMNS], F32, name="lifted")
         nc.vector.tensor_scalar_max(out=lifted[:], in0=magnitude[:], scalar1=SQRT_MIN)
-        root = const.tile([P, UNIT_COLUMNS + ROW_COLUMNS], F32, name="root")
+        root = const.tile([P, P + ROW_COLUMNS], F32, name="root")
         nc.scalar.activation(out=root[:], in_=lifted[:], func=ACT.Sqrt)
-        signs = const.tile([P, UNIT_COLUMNS + ROW_COLUMNS], F32, name="signs")
+        signs = const.tile([P, P + ROW_COLUMNS], F32, name="signs")
         nc.scalar.activation(out=signs[:], in_=draws[:], func=ACT.Sign)
-        factor = const.tile([P, UNIT_COLUMNS + ROW_COLUMNS], F32, name="factor")
-        nc.vector.tensor_mul(out=factor[:], in0=signs[:], in1=root[:])
+        exp_table = const.tile([P, 1], F32, name="exp_table")
+        nc.scalar.activation(out=exp_table[:], in_=signs[:, 0:1], func=ACT.Exp)
+        factor_lines = const.tile([P, P + ROW_COLUMNS], F32, name="factor_lines")
+        nc.vector.tensor_mul(out=factor_lines[:], in0=signs[:], in1=root[:])
+
+        b11_columns = const.tile([P, UNIT_COLUMNS], F32, name="b11_columns")
+        b12_columns = const.tile([P, UNIT_COLUMNS], F32, name="b12_columns")
+        factor = const.tile([P, P], F32, name="factor")
+        nc.vector.memset(factor[:], 0.0)
+        row_factor = const.tile([P, MODULES * ROWS], F32, name="row_factor")
+        parked = out[3, MODULES // 2 :, :].rearrange("j l -> (j l)")
+
+        def turn_small_vectors():
+            lines_f32 = const.tile([P, P], F32, name="lines_f32")
+            nc.vector.tensor_copy(out=lines_f32[:], in_=lines_bf16[:])
+            column_bank = psum.tile([P, 2, P], F32, name="mu", tag="mu")
+            nc.tensor.transpose(column_bank[:, 0, :], factor_lines[:, 0:P], ident[:])
+            nc.tensor.transpose(column_bank[:, 1, :], lines_f32[:], ident[:])
+            nc.vector.tensor_copy(out=factor[:, 0:UNIT_COLUMNS], in_=column_bank[:, 0, 0:UNIT_COLUMNS])
+            nc.vector.tensor_copy(out=b11_columns[:], in_=column_bank[:, 1, 0:UNIT_COLUMNS])
+            nc.vector.tensor_copy(out=b12_columns[:], in_=column_bank[:, 1, UNIT_COLUMNS:P])
+            nc.vector.tensor_copy(
+                out=factor[:, UNIT_COLUMNS : UNIT_COLUMNS + ROW_COLUMNS].rearrange("p (j a) -> p j a", a=ROW_TILES),
+                in_=factor_lines[:, P:].rearrange("p (a j) -> p j a", a=ROW_TILES),
+            )
 
         for q in range(-TRANSPOSE_AHEAD, PAIRS + RELU_BEHIND):
             step_in_module = q % STEPS_PER_MODULE
             coming = q // STEPS_PER_MODULE + 1
-            extra_rows = coming < MODULES and step_in_module < 2
-            extra_factor = coming < MODULES and step_in_module == 3
+            extra_rows = 0 < coming < MODULES and step_in_module < 2
+            first_factor = q == -1
             vector_is_done = q >= PAIRS
 
             if q + TRANSPOSE_AHEAD + LOAD_AHEAD < PAIRS:
                 load_for_pair(q + TRANSPOSE_AHEAD + LOAD_AHEAD)
+
+            if q == -TRANSPOSE_AHEAD:
+                for part in range(2):
+                    transpose_rows(0, part, "backward")
+                    copy_rows(0, part)
 
             if 0 <= q < PAIRS:
                 exponentials(q)
@@ -326,8 +353,8 @@ def tile_skill_net_pa_t_kernel(tc, s, ei1, ej1, w11, b11, w12, b12, out):
                 copy_weights(q + COPY_AHEAD, 0)
             if extra_rows:
                 transpose_rows(coming, step_in_module)
-            if extra_factor:
-                spread_row_factor(coming)
+            if first_factor:
+                spread_first_row_factor()
             if 0 <= q - RELU_BEHIND < PAIRS:
                 relu_out(q - RELU_BEHIND, 0, False)
             if 0 <= q - BACK_BEHIND < PAIRS:
@@ -354,9 +381,13 @@ def tile_skill_net_pa_t_kernel(tc, s, ei1, ej1, w11, b11, w12, b12, out):
                 scale_noise(q)
             if extra_rows:
                 copy_rows(coming, step_in_module)
-            if extra_factor:
-                copy_row_factor(coming)
+            if first_factor:
+                copy_first_row_factor()
             if q + TRANSPOSE_AHEAD < PAIRS:
                 transpose_weights(q + TRANSPOSE_AHEAD, 1)
+            if q == -TRANSPOSE_AHEAD:
+                turn_small_vectors()
+            if q == -2:
+                spread_other_row_factors()
             if 0 <= q < PAIRS:
                 add_mu(q)

@@ -61,6 +61,7 @@ def tile_skill_net_pa_t_kernel(tc, s, ei1, ej1, w11, b11, w12, b12, out):
 
         weight_words = {}
         row_words = {}
+        first_rows = []
         forward_bank = {}
         weight_grouped = {}
         row_grouped = {}
@@ -84,12 +85,12 @@ def tile_skill_net_pa_t_kernel(tc, s, ei1, ej1, w11, b11, w12, b12, out):
             for j in range(count):
                 row_words[first + j] = s_raw[:].bitcast(F32)[:, :, j * WORDS : (j + 1) * WORDS]
 
-        def load_first_rows():
-            s_raw = raw_rows.tile([P, ROW_TILES, 2 * FEATURES], BF16, name="s_raw")
-            for half in range(2):
-                tiles = slice(2 * half, 2 * half + 2)
-                nc.sync.dma_start(out=s_raw[:, tiles, 0:FEATURES], in_=s_view[:, tiles, 0, :])
-            row_words[0] = s_raw[:].bitcast(F32)[:, :, 0:WORDS]
+        def load_first_rows(half):
+            if half == 0:
+                first_rows.append(raw_rows.tile([P, ROW_TILES, 2 * FEATURES], BF16, name="s_raw"))
+                row_words[0] = first_rows[0][:].bitcast(F32)[:, :, 0:WORDS]
+            tiles = slice(2 * half, 2 * half + 2)
+            nc.sync.dma_start(out=first_rows[0][:, tiles, 0:FEATURES], in_=s_view[:, tiles, 0, :])
 
         def load_weights(q):
             j, r = q // STEPS_PER_MODULE, q % STEPS_PER_MODULE
@@ -266,13 +267,18 @@ def tile_skill_net_pa_t_kernel(tc, s, ei1, ej1, w11, b11, w12, b12, out):
             else:
                 nc.scalar.activation(out=out_tile, in_=backward_bank[(q, t)][:], func=ACT.Relu)
 
-        def store(q):
-            one_by_one = q >= PAIRS - 2
-            if q % 2 == 0 and not one_by_one:
+        def store(q, t):
+            if q < PAIRS - 2:
+                tiles = 4 if (q % 2, t) == (1, 1) else 0
+            elif q < PAIRS - 1:
+                tiles = 2 * t
+            else:
+                tiles = 1
+            if tiles == 0:
                 return
-            width = 2 * P if one_by_one else 4 * P
-            last = 2 * P * (q % 2) + 2 * P
-            j, last_unit = q // STEPS_PER_MODULE, 2 * P * (q % STEPS_PER_MODULE) + 2 * P
+            width = tiles * P
+            last = (2 * (q % 2) + t + 1) * P
+            j, last_unit = q // STEPS_PER_MODULE, (2 * (q % STEPS_PER_MODULE) + t + 1) * P
             nc.sync.dma_start(
                 out=out_view[:, :, j, last_unit - width : last_unit],
                 in_=out_pair[q // 2][:, :, last - width : last],
@@ -282,11 +288,12 @@ def tile_skill_net_pa_t_kernel(tc, s, ei1, ej1, w11, b11, w12, b12, out):
         make_identity(nc, ident[:])
 
         draws = const.tile([P, P + ROW_COLUMNS], BF16, name="draws")
-        nc.vector.memset(draws[:], 0.0)
+        nc.vector.memset(draws[UNIT_COLUMNS:P, 0:P], 0.0)
         lines_bf16 = const.tile([P, P], BF16, name="lines_bf16")
+        load_first_rows(0)
         nc.sync.dma_start(out=draws[0:UNIT_COLUMNS, 0:P], in_=ej1.rearrange("o j (g m) -> (o j g) m", m=P))
         nc.sync.dma_start(out=draws[:, P:], in_=ei1.rearrange("(n a) j o -> n (a j o)", a=ROW_TILES))
-        load_first_rows()
+        load_first_rows(1)
         nc.sync.dma_start(out=lines_bf16[0:UNIT_COLUMNS, :], in_=b11.rearrange("j (g m) -> (j g) m", m=P))
         nc.sync.dma_start(out=lines_bf16[UNIT_COLUMNS:P, :], in_=b12.rearrange("j (g m) -> (j g) m", m=P))
         for q in range(LOAD_AHEAD):
@@ -333,7 +340,7 @@ def tile_skill_net_pa_t_kernel(tc, s, ei1, ej1, w11, b11, w12, b12, out):
             coming = q // STEPS_PER_MODULE + 1
             extra_rows = 0 < coming < MODULES and step_in_module < 2
             first_factor = q == -1
-            vector_is_done = q >= PAIRS
+            vector_is_done = q > PAIRS
 
             if q + TRANSPOSE_AHEAD + LOAD_AHEAD < PAIRS:
                 load_for_pair(q + TRANSPOSE_AHEAD + LOAD_AHEAD)
@@ -357,19 +364,19 @@ def tile_skill_net_pa_t_kernel(tc, s, ei1, ej1, w11, b11, w12, b12, out):
                 spread_first_row_factor()
             if 0 <= q - RELU_BEHIND < PAIRS:
                 relu_out(q - RELU_BEHIND, 0, False)
+                store(q - RELU_BEHIND, 0)
             if 0 <= q - BACK_BEHIND < PAIRS:
                 transpose_back(q - BACK_BEHIND, 0)
+            if 0 <= q < PAIRS:
+                multiply(q, 1, mu_bank, "mu")
             if 0 <= q + COPY_AHEAD < PAIRS:
                 copy_weights(q + COPY_AHEAD, 1)
             if q + TRANSPOSE_AHEAD < PAIRS:
                 transpose_weights(q + TRANSPOSE_AHEAD, 0)
 
-            if 0 <= q < PAIRS:
-                multiply(q, 1, mu_bank, "mu")
-
             if 0 <= q - RELU_BEHIND < PAIRS:
                 relu_out(q - RELU_BEHIND, 1, vector_is_done)
-                store(q - RELU_BEHIND)
+                store(q - RELU_BEHIND, 1)
             if 0 <= q - BACK_BEHIND < PAIRS:
                 transpose_back(q - BACK_BEHIND, 1)
 

@@ -34,8 +34,8 @@ ROW_COLUMNS = ROW_TILES * MODULES
 TRANSPOSE_AHEAD = 4
 COPY_AHEAD = 3
 QUANTISE_AHEAD = 2
-BACK_BEHIND = 1
 RELU_BEHIND = 2
+TURNED_BANKS = 3
 LOAD_AHEAD = 6
 
 FLOPS = 2 * 2 * MODULES * ROWS * UNITS * FEATURES
@@ -54,7 +54,7 @@ def tile_skill_net_pa_t_kernel(tc, s, ei1, ej1, w11, b11, w12, b12, out):
         raw_rows = stack.enter_context(tc.tile_pool(name="raw_rows", bufs=3))
         grouped = stack.enter_context(tc.tile_pool(name="grouped", bufs=3))
         packed = stack.enter_context(tc.tile_pool(name="packed", bufs=4))
-        work = stack.enter_context(tc.tile_pool(name="work", bufs=3))
+        work = stack.enter_context(tc.tile_pool(name="work", bufs=4))
         result = stack.enter_context(tc.tile_pool(name="result", bufs=4))
         psum = stack.enter_context(tc.psum_pool(name="psum", bufs=2))
         stack.enter_context(tc.manual_schedule())
@@ -69,6 +69,7 @@ def tile_skill_net_pa_t_kernel(tc, s, ei1, ej1, w11, b11, w12, b12, out):
         weight_scales = {}
         row_codes = {}
         row_scales = {}
+        row_factor = {}
         log_sigma_bank = {}
         mu_bank = {}
         sigma = {}
@@ -111,8 +112,7 @@ def tile_skill_net_pa_t_kernel(tc, s, ei1, ej1, w11, b11, w12, b12, out):
                 load_rows(q // STEPS_PER_MODULE + 1, 2)
             load_weights(q)
 
-        def transpose_two_tiles(tiles, key, tag="forward"):
-            bank = psum.tile([P, 2, 2, P], F32, name=tag, tag=tag)
+        def transpose_two_tiles(tiles, key, bank):
             for t in range(2):
                 for u in range(2):
                     nc.tensor.transpose(bank[:, t, u, :], tiles[t][:, u * P : (u + 1) * P], ident[:])
@@ -121,7 +121,8 @@ def tile_skill_net_pa_t_kernel(tc, s, ei1, ej1, w11, b11, w12, b12, out):
         def transpose_weights(q, x):
             first = 2 * x * WORDS
             tiles = [weight_words[q][:, first + t * WORDS : first + (t + 1) * WORDS] for t in range(2)]
-            transpose_two_tiles(tiles, ("w", q, x))
+            bank = psum.tile([P, 2, 2, P], F32, name="turned", tag="turned", bufs=TURNED_BANKS)
+            transpose_two_tiles(tiles, ("w", q, x), bank)
 
         def copy_weights(q, x):
             if x == 0:
@@ -144,9 +145,10 @@ def tile_skill_net_pa_t_kernel(tc, s, ei1, ej1, w11, b11, w12, b12, out):
                 in_=weight_grouped[q][:],
             )
 
-        def transpose_rows(j, half, tag="forward"):
+        def transpose_rows(j, half):
             tiles = [row_words[j][:, 2 * half + t, :] for t in range(2)]
-            transpose_two_tiles(tiles, ("s", j, half), tag)
+            bank = psum.tile([P, 2, 2, P], F32, name="mu", tag="mu")
+            transpose_two_tiles(tiles, ("s", j, half), bank)
 
         def copy_rows(j, half):
             if half == 0:
@@ -166,28 +168,14 @@ def tile_skill_net_pa_t_kernel(tc, s, ei1, ej1, w11, b11, w12, b12, out):
                 in_=row_grouped[j][:],
             )
 
-        def spread_first_row_factor():
-            bank = psum.tile([P, ROW_TILES, P], F32, name="forward", tag="forward")
+        def spread_row_factor(j):
+            bank = psum.tile([P, ROW_TILES, P], F32, name="row_factor", tag="row_factor", bufs=1)
             for a in range(ROW_TILES):
-                column = UNIT_COLUMNS + a
+                column = P + a * MODULES + j
                 nc.tensor.transpose(
-                    bank[:, a, :], factor[:, column : column + 1].to_broadcast([P, P]), ident[:]
+                    bank[:, a, :], factor_lines[:, column : column + 1].to_broadcast([P, P]), ident[:]
                 )
-            forward_bank["f"] = bank
-
-        def copy_first_row_factor():
-            nc.vector.tensor_copy(
-                out=row_factor[:, 0:ROWS], in_=forward_bank["f"][:].rearrange("p a n -> p (a n)")
-            )
-
-        def spread_other_row_factors():
-            bank = psum.tile([P, P], F32, name="backward", tag="backward")
-            nc.tensor.transpose(bank[:], factor[:], ident[:])
-            line_pieces = const.tile([P, P], F32, name="line_pieces")
-            pieces = slice(UNIT_COLUMNS, UNIT_COLUMNS + ROW_COLUMNS)
-            nc.vector.tensor_copy(out=line_pieces[pieces, :], in_=bank[pieces, :])
-            nc.sync.dma_start(out=parked.rearrange("(c n) -> c n", n=P), in_=line_pieces[pieces, :])
-            nc.sync.dma_start(out=row_factor[:, ROWS:], in_=parked[ROWS:].partition_broadcast(P))
+            row_factor[j] = bank[:].rearrange("p a n -> p (a n)")
 
         def multiply(q, x, banks, tag):
             j = q // STEPS_PER_MODULE
@@ -205,59 +193,57 @@ def tile_skill_net_pa_t_kernel(tc, s, ei1, ej1, w11, b11, w12, b12, out):
                 )
                 banks[(q, t)] = bank
 
-        def exponentials(q):
-            sigma[q] = work.tile([P, 2, ROWS], F32, name="sigma")
-            for t in range(2):
-                nc.scalar.activation(
-                    out=sigma[q][:, t, :],
-                    in_=log_sigma_bank[(q, t)][:],
-                    func=ACT.Exp,
-                    bias=b12_columns[:, 2 * q + t : 2 * q + t + 1],
-                    scale=1.0,
-                )
+        def exponential(q, t):
+            if t == 0:
+                sigma[q] = work.tile([P, 2, ROWS], F32, name="sigma")
+            nc.scalar.activation(
+                out=sigma[q][:, t, :],
+                in_=log_sigma_bank[(q, t)][:],
+                func=ACT.Exp,
+                bias=b12_columns[:, 2 * q + t : 2 * q + t + 1],
+                scale=1.0,
+            )
 
-        def clip_sigma(q):
-            for t in range(2):
-                nc.gpsimd.tensor_scalar(
-                    out=sigma[q][:, t, :],
-                    in0=sigma[q][:, t, :],
-                    scalar1=SIGMA_MAX,
-                    scalar2=SIGMA_MIN,
-                    op0=ALU.min,
-                    op1=ALU.max,
-                )
+        def clip_sigma(q, t):
+            nc.gpsimd.tensor_scalar(
+                out=sigma[q][:, t, :],
+                in0=sigma[q][:, t, :],
+                scalar1=SIGMA_MAX,
+                scalar2=SIGMA_MIN,
+                op0=ALU.min,
+                op1=ALU.max,
+            )
 
-        def scale_noise(q):
-            j = q // STEPS_PER_MODULE
-            for t in range(2):
-                nc.vector.scalar_tensor_tensor(
-                    out=sigma[q][:, t, :],
-                    in0=sigma[q][:, t, :],
-                    scalar=factor[:, 2 * q + t : 2 * q + t + 1],
-                    in1=row_factor[:, j * ROWS : (j + 1) * ROWS],
-                    op0=ALU.mult,
-                    op1=ALU.mult,
-                )
+        def scale_noise(q, t):
+            nc.vector.scalar_tensor_tensor(
+                out=sigma[q][:, t, :],
+                in0=sigma[q][:, t, :],
+                scalar=factor[:, 2 * q + t : 2 * q + t + 1],
+                in1=row_factor[q // STEPS_PER_MODULE],
+                op0=ALU.mult,
+                op1=ALU.mult,
+            )
 
-        def add_mu(q):
-            summed[q] = work.tile([P, 2, ROWS], F32, name="summed")
-            for t in range(2):
-                nc.vector.scalar_tensor_tensor(
-                    out=summed[q][:, t, :],
-                    in0=mu_bank[(q, t)][:],
-                    scalar=b11_columns[:, 2 * q + t : 2 * q + t + 1],
-                    in1=sigma[q][:, t, :],
-                    op0=ALU.add,
-                    op1=ALU.add,
-                )
+        def add_mu(q, t):
+            if t == 0:
+                summed[q] = work.tile([P, 2, ROWS], F32, name="summed")
+            nc.vector.scalar_tensor_tensor(
+                out=summed[q][:, t, :],
+                in0=mu_bank[(q, t)][:],
+                scalar=b11_columns[:, 2 * q + t : 2 * q + t + 1],
+                in1=sigma[q][:, t, :],
+                op0=ALU.add,
+                op1=ALU.add,
+            )
 
         def transpose_back(q, t):
-            bank = psum.tile([P, ROW_TILES, P], F32, name="backward", tag="backward")
+            bank = psum.tile([P, ROW_TILES, P], F32, name="turned", tag="turned", bufs=TURNED_BANKS)
             for a in range(ROW_TILES):
                 nc.tensor.transpose(bank[:, a, :], summed[q][:, t, a * P : (a + 1) * P], ident[:])
             backward_bank[(q, t)] = bank
 
-        def relu_out(q, t, on_vector):
+        def relu_out(q, t):
+            on_vector = (q, t) == (PAIRS - 1, 1)
             if t == 0 and q % 2 == 0:
                 out_pair[q // 2] = result.tile([P, ROW_TILES, 4 * P], F32, name="out_pair")
             first = (2 * (q % 2) + t) * P
@@ -283,6 +269,9 @@ def tile_skill_net_pa_t_kernel(tc, s, ei1, ej1, w11, b11, w12, b12, out):
                 out=out_view[:, :, j, last_unit - width : last_unit],
                 in_=out_pair[q // 2][:, :, last - width : last],
             )
+
+        def within(q):
+            return 0 <= q < PAIRS
 
         ident = const.tile([P, P], F32, name="ident")
         make_identity(nc, ident[:])
@@ -316,85 +305,74 @@ def tile_skill_net_pa_t_kernel(tc, s, ei1, ej1, w11, b11, w12, b12, out):
 
         b11_columns = const.tile([P, UNIT_COLUMNS], F32, name="b11_columns")
         b12_columns = const.tile([P, UNIT_COLUMNS], F32, name="b12_columns")
-        factor = const.tile([P, P], F32, name="factor")
-        nc.vector.memset(factor[:], 0.0)
-        row_factor = const.tile([P, MODULES * ROWS], F32, name="row_factor")
-        parked = out[3, MODULES // 2 :, :].rearrange("j l -> (j l)")
+        factor = const.tile([P, UNIT_COLUMNS], F32, name="factor")
 
         def turn_small_vectors():
             lines_f32 = const.tile([P, P], F32, name="lines_f32")
             nc.vector.tensor_copy(out=lines_f32[:], in_=lines_bf16[:])
-            column_bank = psum.tile([P, 2, P], F32, name="mu", tag="mu")
+            column_bank = psum.tile([P, 2, P], F32, name="log_sigma", tag="log_sigma")
             nc.tensor.transpose(column_bank[:, 0, :], factor_lines[:, 0:P], ident[:])
             nc.tensor.transpose(column_bank[:, 1, :], lines_f32[:], ident[:])
-            nc.vector.tensor_copy(out=factor[:, 0:UNIT_COLUMNS], in_=column_bank[:, 0, 0:UNIT_COLUMNS])
+            nc.vector.tensor_copy(out=factor[:], in_=column_bank[:, 0, 0:UNIT_COLUMNS])
             nc.vector.tensor_copy(out=b11_columns[:], in_=column_bank[:, 1, 0:UNIT_COLUMNS])
             nc.vector.tensor_copy(out=b12_columns[:], in_=column_bank[:, 1, UNIT_COLUMNS:P])
-            nc.vector.tensor_copy(
-                out=factor[:, UNIT_COLUMNS : UNIT_COLUMNS + ROW_COLUMNS].rearrange("p (j a) -> p j a", a=ROW_TILES),
-                in_=factor_lines[:, P:].rearrange("p (a j) -> p j a", a=ROW_TILES),
-            )
 
         for q in range(-TRANSPOSE_AHEAD, PAIRS + RELU_BEHIND):
             step_in_module = q % STEPS_PER_MODULE
             coming = q // STEPS_PER_MODULE + 1
             extra_rows = 0 < coming < MODULES and step_in_module < 2
-            first_factor = q == -1
-            vector_is_done = q > PAIRS
 
-            if q + TRANSPOSE_AHEAD + LOAD_AHEAD < PAIRS:
+            if within(q + TRANSPOSE_AHEAD + LOAD_AHEAD):
                 load_for_pair(q + TRANSPOSE_AHEAD + LOAD_AHEAD)
-
             if q == -TRANSPOSE_AHEAD:
                 for part in range(2):
-                    transpose_rows(0, part, "backward")
+                    transpose_rows(0, part)
                     copy_rows(0, part)
 
-            if 0 <= q < PAIRS:
-                exponentials(q)
-                clip_sigma(q)
-            if 0 <= q + 1 < PAIRS:
-                multiply(q + 1, 0, log_sigma_bank, "log_sigma")
-
-            if 0 <= q + COPY_AHEAD < PAIRS:
+            if within(q + COPY_AHEAD):
                 copy_weights(q + COPY_AHEAD, 0)
+            if within(q):
+                exponential(q, 0)
+                clip_sigma(q, 0)
+            if within(q - 1):
+                scale_noise(q - 1, 1)
+                add_mu(q - 1, 0)
+            if within(q - RELU_BEHIND):
+                transpose_back(q - RELU_BEHIND, 1)
+            if within(q) and step_in_module == 0:
+                spread_row_factor(q // STEPS_PER_MODULE)
+            if within(q - RELU_BEHIND):
+                relu_out(q - RELU_BEHIND, 0)
+                store(q - RELU_BEHIND, 0)
+            if within(q + TRANSPOSE_AHEAD):
+                transpose_weights(q + TRANSPOSE_AHEAD, 0)
+            if within(q + COPY_AHEAD):
+                copy_weights(q + COPY_AHEAD, 1)
+            if within(q - 1):
+                transpose_back(q - 1, 0)
             if extra_rows:
                 transpose_rows(coming, step_in_module)
-            if first_factor:
-                spread_first_row_factor()
-            if 0 <= q - RELU_BEHIND < PAIRS:
-                relu_out(q - RELU_BEHIND, 0, False)
-                store(q - RELU_BEHIND, 0)
-            if 0 <= q - BACK_BEHIND < PAIRS:
-                transpose_back(q - BACK_BEHIND, 0)
-            if 0 <= q < PAIRS:
-                multiply(q, 1, mu_bank, "mu")
-            if 0 <= q + COPY_AHEAD < PAIRS:
-                copy_weights(q + COPY_AHEAD, 1)
-            if q + TRANSPOSE_AHEAD < PAIRS:
-                transpose_weights(q + TRANSPOSE_AHEAD, 0)
-
-            if 0 <= q - RELU_BEHIND < PAIRS:
-                relu_out(q - RELU_BEHIND, 1, vector_is_done)
+            if within(q):
+                exponential(q, 1)
+                clip_sigma(q, 1)
+            if within(q + 1):
+                multiply(q + 1, 0, log_sigma_bank, "log_sigma")
+            if within(q - RELU_BEHIND):
+                relu_out(q - RELU_BEHIND, 1)
                 store(q - RELU_BEHIND, 1)
-            if 0 <= q - BACK_BEHIND < PAIRS:
-                transpose_back(q - BACK_BEHIND, 1)
-
-            if 0 <= q + QUANTISE_AHEAD < PAIRS:
-                quantise_weights(q + QUANTISE_AHEAD)
-            if coming < MODULES and step_in_module == 2:
-                quantise_rows(coming)
-            if 0 <= q < PAIRS:
-                scale_noise(q)
-            if extra_rows:
-                copy_rows(coming, step_in_module)
-            if first_factor:
-                copy_first_row_factor()
-            if q + TRANSPOSE_AHEAD < PAIRS:
+            if within(q + TRANSPOSE_AHEAD):
                 transpose_weights(q + TRANSPOSE_AHEAD, 1)
             if q == -TRANSPOSE_AHEAD:
                 turn_small_vectors()
-            if q == -2:
-                spread_other_row_factors()
-            if 0 <= q < PAIRS:
-                add_mu(q)
+            if within(q + QUANTISE_AHEAD):
+                quantise_weights(q + QUANTISE_AHEAD)
+            if coming < MODULES and step_in_module == 2:
+                quantise_rows(coming)
+            if within(q):
+                scale_noise(q, 0)
+            if within(q - 1):
+                add_mu(q - 1, 1)
+            if extra_rows:
+                copy_rows(coming, step_in_module)
+            if within(q):
+                multiply(q, 1, mu_bank, "mu")

import math
from contextlib import ExitStack

import concourse.mybir as mybir
from concourse.masks import make_identity

F32 = mybir.dt.float32
BF16 = mybir.dt.bfloat16
U32 = mybir.dt.uint32
U8 = mybir.dt.uint8
FP8X4 = mybir.dt.float8_e4m3fn_x4
ACT = mybir.ActivationFunctionType
ALU = mybir.AluOpType

P = 128
PACK = 4
MODULES = 8
ROWS = 512
FEATURES = 512
UNITS = 1024
ROW_TILES = ROWS // P
UNIT_TILES = UNITS // P
WORDS = FEATURES // 2
STEPS_PER_MODULE = UNIT_TILES // 2
PAIRS = MODULES * STEPS_PER_MODULE

SIGMA_MAX = math.exp(4.0)
SIGMA_MIN = math.exp(-20.0)
SQRT_MIN = 2.0**-116

UNIT_COLUMNS = MODULES * UNIT_TILES
ROW_COLUMNS = ROW_TILES * MODULES

TRANSPOSE_AHEAD = 4
COPY_AHEAD = 3
QUANTISE_AHEAD = 2
RELU_BEHIND = 2
TURNED_BANKS = 3
LOAD_AHEAD = 6

FLOPS = 2 * 2 * MODULES * ROWS * UNITS * FEATURES


def tile_skill_net_pa_t_kernel(tc, s, ei1, ej1, w11, b11, w12, b12, out):
    nc = tc.nc

    s_view = s.rearrange("(n a) j k -> n a j k", a=ROW_TILES)
    w_views = [w.rearrange("j (r m t) k -> j r m t k", m=P, t=2) for w in (w12, w11)]
    out_view = out.rearrange("(n a) j l -> n a j l", a=ROW_TILES)

    with ExitStack() as stack:
        const = stack.enter_context(tc.tile_pool(name="const", bufs=1))
        raw_weights = stack.enter_context(tc.tile_pool(name="raw_weights", bufs=LOAD_AHEAD + 2))
        raw_rows = stack.enter_context(tc.tile_pool(name="raw_rows", bufs=3))
        grouped = stack.enter_context(tc.tile_pool(name="grouped", bufs=3))
        packed = stack.enter_context(tc.tile_pool(name="packed", bufs=4))
        work = stack.enter_context(tc.tile_pool(name="work", bufs=4))
        result = stack.enter_context(tc.tile_pool(name="result", bufs=4))
        psum = stack.enter_context(tc.psum_pool(name="psum", bufs=2))
        stack.enter_context(tc.manual_schedule())

        weight_words = {}
        row_words = {}
        first_rows = []
        forward_bank = {}
        weight_grouped = {}
        row_grouped = {}
        weight_codes = {}
        weight_scales = {}
        row_codes = {}
        row_scales = {}
        row_factor = {}
        log_sigma_bank = {}
        mu_bank = {}
        sigma = {}
        summed = {}
        backward_bank = {}
        out_pair = {}

        def load_rows(first, count):
            s_raw = raw_rows.tile([P, ROW_TILES, 2 * FEATURES], BF16, name="s_raw")
            nc.sync.dma_start(
                out=s_raw[:, :, 0 : count * FEATURES],
                in_=s_view[:, :, first : first + count, :].rearrange("n a j k -> n a (j k)"),
            )
            for j in range(count):
                row_words[first + j] = s_raw[:].bitcast(F32)[:, :, j * WORDS : (j + 1) * WORDS]

        def load_first_rows(half):
            if half == 0:
                first_rows.append(raw_rows.tile([P, ROW_TILES, 2 * FEATURES], BF16, name="s_raw"))
                row_words[0] = first_rows[0][:].bitcast(F32)[:, :, 0:WORDS]
            tiles = slice(2 * half, 2 * half + 2)
            nc.sync.dma_start(out=first_rows[0][:, tiles, 0:FEATURES], in_=s_view[:, tiles, 0, :])

        def load_weights(q):
            j, r = q // STEPS_PER_MODULE, q % STEPS_PER_MODULE
            w_raw = raw_weights.tile([P, 2 * 2 * FEATURES], BF16, name="w_raw")
            for x in range(2):
                nc.sync.dma_start(
                    out=w_raw[:, x * 2 * FEATURES : (x + 1) * 2 * FEATURES].rearrange(
                        "p (t k) -> p t k", t=2
                    ),
                    in_=w_views[x][j, r],
                )
            weight_words[q] = w_raw[:].bitcast(F32)

        def load_for_pair(q):
            if q == 2:
                load_rows(1, 1)
            elif q % (2 * STEPS_PER_MODULE) == STEPS_PER_MODULE and q < PAIRS - STEPS_PER_MODULE:
                load_rows(q // STEPS_PER_MODULE + 1, 2)
            load_weights(q)

        def transpose_two_tiles(tiles, key, bank):
            for t in range(2):
                for u in range(2):
                    nc.tensor.transpose(bank[:, t, u, :], tiles[t][:, u * P : (u + 1) * P], ident[:])
            forward_bank[key] = bank

        def transpose_weights(q, x):
            first = 2 * x * WORDS
            tiles = [weight_words[q][:, first + t * WORDS : first + (t + 1) * WORDS] for t in range(2)]
            bank = psum.tile([P, 2, 2, P], F32, name="turned", tag="turned", bufs=TURNED_BANKS)
            transpose_two_tiles(tiles, ("w", q, x), bank)

        def copy_weights(q, x):
            if x == 0:
                weight_grouped[q] = grouped.tile(
                    [P, 2 * 2 * P * PACK], BF16, name="w_grouped", align_bytes=64
                )
            view = weight_grouped[q][:].bitcast(F32).rearrange(
                "p (x m t u) -> p x m t u", x=2, t=2, u=2
            )
            nc.scalar.copy(
                out=view[:, x], in_=forward_bank[("w", q, x)][:].rearrange("p t u m -> p m t u")
            )

        def quantise_weights(q):
            weight_codes[q] = packed.tile([P, 2 * 2 * P], U32, name="w_codes", align_bytes=64)
            weight_scales[q] = packed.tile([P, 2 * 2 * P], U8, name="w_scales", align_bytes=64)
            nc.vector.quantize_mx(
                out=weight_codes[q][:].bitcast(FP8X4),
                scales=weight_scales[q][:],
                in_=weight_grouped[q][:],
            )

        def transpose_rows(j, half):
            tiles = [row_words[j][:, 2 * half + t, :] for t in range(2)]
            bank = psum.tile([P, 2, 2, P], F32, name="mu", tag="mu")
            transpose_two_tiles(tiles, ("s", j, half), bank)

        def copy_rows(j, half):
            if half == 0:
                row_grouped[j] = grouped.tile([P, ROWS * PACK], BF16, name="s_grouped", align_bytes=64)
            view = row_grouped[j][:].bitcast(F32).rearrange("p (a n u) -> p a n u", a=ROW_TILES, u=2)
            nc.vector.tensor_copy(
                out=view[:, 2 * half : 2 * half + 2],
                in_=forward_bank[("s", j, half)][:].rearrange("p t u r -> p t r u"),
            )

        def quantise_rows(j):
            row_codes[j] = packed.tile([P, ROWS], U32, name="s_codes", align_bytes=64)
            row_scales[j] = packed.tile([P, ROWS], U8, name="s_scales", align_bytes=64)
            nc.vector.quantize_mx(
                out=row_codes[j][:].bitcast(FP8X4),
                scales=row_scales[j][:],
                in_=row_grouped[j][:],
            )

        def spread_row_factor(j):
            bank = psum.tile([P, ROW_TILES, P], F32, name="row_factor", tag="row_factor", bufs=1)
            for a in range(ROW_TILES):
                column = P + a * MODULES + j
                nc.tensor.transpose(
                    bank[:, a, :], factor_lines[:, column : column + 1].to_broadcast([P, P]), ident[:]
                )
            row_factor[j] = bank[:].rearrange("p a n -> p (a n)")

        def multiply(q, x, banks, tag):
            j = q // STEPS_PER_MODULE
            for t in range(2):
                bank = psum.tile([P, ROWS], F32, name=tag, tag=tag)
                tile_columns = slice((2 * x + t) * P, (2 * x + t + 1) * P)
                nc.tensor.matmul_mx(
                    out=bank[:],
                    lhsT=weight_codes[q][:, tile_columns].bitcast(FP8X4),
                    lhsT_scale=weight_scales[q][:, tile_columns],
                    rhs=row_codes[j][:].bitcast(FP8X4),
                    rhs_scale=row_scales[j][:],
                    start=True,
                    stop=True,
                )
                banks[(q, t)] = bank

        def exponential(q, t):
            if t == 0:
                sigma[q] = work.tile([P, 2, ROWS], F32, name="sigma")
            nc.scalar.activation(
                out=sigma[q][:, t, :],
                in_=log_sigma_bank[(q, t)][:],
                func=ACT.Exp,
                bias=b12_columns[:, 2 * q + t : 2 * q + t + 1],
                scale=1.0,
            )

        def clip_sigma(q, t):
            nc.gpsimd.tensor_scalar(
                out=sigma[q][:, t, :],
                in0=sigma[q][:, t, :],
                scalar1=SIGMA_MAX,
                scalar2=SIGMA_MIN,
                op0=ALU.min,
                op1=ALU.max,
            )

        def scale_noise(q, t):
            nc.vector.scalar_tensor_tensor(
                out=sigma[q][:, t, :],
                in0=sigma[q][:, t, :],
                scalar=factor[:, 2 * q + t : 2 * q + t + 1],
                in1=row_factor[q // STEPS_PER_MODULE],
                op0=ALU.mult,
                op1=ALU.mult,
            )

        def add_mu(q, t):
            if t == 0:
                summed[q] = work.tile([P, 2, ROWS], F32, name="summed")
            nc.vector.scalar_tensor_tensor(
                out=summed[q][:, t, :],
                in0=mu_bank[(q, t)][:],
                scalar=b11_columns[:, 2 * q + t : 2 * q + t + 1],
                in1=sigma[q][:, t, :],
                op0=ALU.add,
                op1=ALU.add,
            )

        def transpose_back(q, t):
            bank = psum.tile([P, ROW_TILES, P], F32, name="turned", tag="turned", bufs=TURNED_BANKS)
            for a in range(ROW_TILES):
                nc.tensor.transpose(bank[:, a, :], summed[q][:, t, a * P : (a + 1) * P], ident[:])
            backward_bank[(q, t)] = bank

        def relu_out(q, t):
            on_vector = (q, t) == (PAIRS - 1, 1)
            if t == 0 and q % 2 == 0:
                out_pair[q // 2] = result.tile([P, ROW_TILES, 4 * P], F32, name="out_pair")
            first = (2 * (q % 2) + t) * P
            out_tile = out_pair[q // 2][:, :, first : first + P]
            if on_vector:
                nc.vector.tensor_scalar_max(out=out_tile, in0=backward_bank[(q, t)][:], scalar1=0.0)
            else:
                nc.scalar.activation(out=out_tile, in_=backward_bank[(q, t)][:], func=ACT.Relu)

        def store(q, t):
            if q < PAIRS - 2:
                tiles = 4 if (q % 2, t) == (1, 1) else 0
            elif q < PAIRS - 1:
                tiles = 2 * t
            else:
                tiles = 1
            if tiles == 0:
                return
            width = tiles * P
            last = (2 * (q % 2) + t + 1) * P
            j, last_unit = q // STEPS_PER_MODULE, (2 * (q % STEPS_PER_MODULE) + t + 1) * P
            nc.sync.dma_start(
                out=out_view[:, :, j, last_unit - width : last_unit],
                in_=out_pair[q // 2][:, :, last - width : last],
            )

        def within(q):
            return 0 <= q < PAIRS

        ident = const.tile([P, P], F32, name="ident")
        make_identity(nc, ident[:])

        draws = const.tile([P, P + ROW_COLUMNS], BF16, name="draws")
        nc.vector.memset(draws[UNIT_COLUMNS:P, 0:P], 0.0)
        lines_bf16 = const.tile([P, P], BF16, name="lines_bf16")
        load_first_rows(0)
        nc.sync.dma_start(out=draws[0:UNIT_COLUMNS, 0:P], in_=ej1.rearrange("o j (g m) -> (o j g) m", m=P))
        nc.sync.dma_start(out=draws[:, P:], in_=ei1.rearrange("(n a) j o -> n (a j o)", a=ROW_TILES))
        load_first_rows(1)
        nc.sync.dma_start(out=lines_bf16[0:UNIT_COLUMNS, :], in_=b11.rearrange("j (g m) -> (j g) m", m=P))
        nc.sync.dma_start(out=lines_bf16[UNIT_COLUMNS:P, :], in_=b12.rearrange("j (g m) -> (j g) m", m=P))
        for q in range(LOAD_AHEAD):
            load_for_pair(q)

        magnitude = const.tile([P, P + ROW_COLUMNS], F32, name="magnitude")
        nc.vector.scalar_tensor_tensor(
            out=magnitude[:], in0=draws[:], scalar=-1.0, in1=draws[:], op0=ALU.mult, op1=ALU.max
        )
        lifted = const.tile([P, P + ROW_COLUMNS], F32, name="lifted")
        nc.vector.tensor_scalar_max(out=lifted[:], in0=magnitude[:], scalar1=SQRT_MIN)
        root = const.tile([P, P + ROW_COLUMNS], F32, name="root")
        nc.scalar.activation(out=root[:], in_=lifted[:], func=ACT.Sqrt)
        signs = const.tile([P, P + ROW_COLUMNS], F32, name="signs")
        nc.scalar.activation(out=signs[:], in_=draws[:], func=ACT.Sign)
        exp_table = const.tile([P, 1], F32, name="exp_table")
        nc.scalar.activation(out=exp_table[:], in_=signs[:, 0:1], func=ACT.Exp)
        factor_lines = const.tile([P, P + ROW_COLUMNS], F32, name="factor_lines")
        nc.vector.tensor_mul(out=factor_lines[:], in0=signs[:], in1=root[:])

        b11_columns = const.tile([P, UNIT_COLUMNS], F32, name="b11_columns")
        b12_columns = const.tile([P, UNIT_COLUMNS], F32, name="b12_columns")
        factor = const.tile([P, UNIT_COLUMNS], F32, name="factor")

        def turn_small_vectors():
            lines_f32 = const.tile([P, P], F32, name="lines_f32")
            nc.vector.tensor_copy(out=lines_f32[:], in_=lines_bf16[:])
            column_bank = psum.tile([P, 2, P], F32, name="log_sigma", tag="log_sigma")
            nc.tensor.transpose(column_bank[:, 0, :], factor_lines[:, 0:P], ident[:])
            nc.tensor.transpose(column_bank[:, 1, :], lines_f32[:], ident[:])
            nc.vector.tensor_copy(out=factor[:], in_=column_bank[:, 0, 0:UNIT_COLUMNS])
            nc.vector.tensor_copy(out=b11_columns[:], in_=column_bank[:, 1, 0:UNIT_COLUMNS])
            nc.vector.tensor_copy(out=b12_columns[:], in_=column_bank[:, 1, UNIT_COLUMNS:P])

        for q in range(-TRANSPOSE_AHEAD, PAIRS + RELU_BEHIND):
            step_in_module = q % STEPS_PER_MODULE
            coming = q // STEPS_PER_MODULE + 1
            extra_rows = 0 < coming < MODULES and step_in_module < 2

            if within(q + TRANSPOSE_AHEAD + LOAD_AHEAD):
                load_for_pair(q + TRANSPOSE_AHEAD + LOAD_AHEAD)
            if q == -TRANSPOSE_AHEAD:
                for part in range(2):
                    transpose_rows(0, part)
                    copy_rows(0, part)

            if within(q + COPY_AHEAD):
                copy_weights(q + COPY_AHEAD, 0)
            if within(q):
                exponential(q, 0)
                clip_sigma(q, 0)
            if within(q - 1):
                scale_noise(q - 1, 1)
                add_mu(q - 1, 0)
            if within(q - RELU_BEHIND):
                transpose_back(q - RELU_BEHIND, 1)
            if within(q) and step_in_module == 0:
                spread_row_factor(q // STEPS_PER_MODULE)
            if within(q - RELU_BEHIND):
                relu_out(q - RELU_BEHIND, 0)
                store(q - RELU_BEHIND, 0)
            if within(q + TRANSPOSE_AHEAD):
                transpose_weights(q + TRANSPOSE_AHEAD, 0)
            if within(q + COPY_AHEAD):
                copy_weights(q + COPY_AHEAD, 1)
            if within(q - 1):
                transpose_back(q - 1, 0)
            if extra_rows:
                transpose_rows(coming, step_in_module)
            if within(q):
                exponential(q, 1)
                clip_sigma(q, 1)
            if within(q + 1):
                multiply(q + 1, 0, log_sigma_bank, "log_sigma")
            if within(q - RELU_BEHIND):
                relu_out(q - RELU_BEHIND, 1)
                store(q - RELU_BEHIND, 1)
            if within(q + TRANSPOSE_AHEAD):
                transpose_weights(q + TRANSPOSE_AHEAD, 1)
            if q == -TRANSPOSE_AHEAD:
                turn_small_vectors()
            if within(q + QUANTISE_AHEAD):
                quantise_weights(q + QUANTISE_AHEAD)
            if coming < MODULES and step_in_module == 2:
                quantise_rows(coming)
            if within(q):
                scale_noise(q, 0)
            if within(q - 1):
                add_mu(q - 1, 1)
            if extra_rows:
                copy_rows(coming, step_in_module)
            if within(q):
                multiply(q, 1, mu_bank, "mu")
